import numpy as np
import ml_dtypes


def mxq(x, axis, fmt="e4m3"):
    dtype, down = {"e4m3": (ml_dtypes.float8_e4m3fn, 7), "e5m2": (ml_dtypes.float8_e5m2, 14)}[fmt]
    v = np.moveaxis(np.asarray(x, np.float32).astype(ml_dtypes.bfloat16).astype(np.float64), axis, -1)
    blocks = v.reshape(v.shape[:-1] + (-1, 32))
    amax = np.abs(blocks).max(-1, keepdims=True)
    byte = np.maximum(np.where(amax > 0, np.frexp(amax)[1] - 1 + 127, 0) - down, 1)
    scale = np.exp2(byte - 127.0)
    codes = (blocks / scale).astype(np.float32).astype(dtype).astype(np.float64)
    return np.moveaxis((codes * scale).reshape(v.shape), -1, axis)


WIDE = False


def mx_kscale(k):
    if not WIDE:
        return np.ones(k)
    levels = np.array([10, -10, 5, -5, 0])
    a = np.random.permutation(np.resize(levels, k // 512 * 4)).reshape(k // 512, 4)
    idx = np.arange(k)
    return np.exp2(a[idx // 512, idx % 128 // 32])


BF16 = ml_dtypes.bfloat16


def bf(x):
    return np.asarray(x, np.float32).astype(BF16)


def f64(x):
    return np.asarray(x).astype(np.float64)


E2M1 = np.array([0.0, 0.5, 1.0, 1.5, 2.0, 3.0, 4.0, 6.0, -0.0, -0.5, -1.0, -1.5, -2.0, -3.0, -4.0, -6.0])


def pack_weight(w, fmt):
    k, n = w.shape
    w = f64(bf(w)).reshape(k // 32, 32, n)
    amax = np.abs(w).max(1)
    if fmt == "e4m3":
        byte = np.frexp(amax)[1] - 1 + 127 - 7
    else:
        mant, ex = np.frexp(amax / 6.0)
        byte = np.where(mant > 0.5, ex, ex - 1) + 127
    byte = np.clip(np.where(amax > 0, byte, 1), 1, 254)
    scaled = (w * np.exp2(127.0 - byte)[:, None, :]).reshape(k, n).astype(np.float32)
    by_word = np.ascontiguousarray(scaled.reshape(k // 512, 128, 4, n).transpose(0, 1, 3, 2))
    if fmt == "e4m3":
        words = by_word.astype(ml_dtypes.float8_e4m3fn).view(np.uint8)
    else:
        c = by_word.astype(ml_dtypes.float4_e2m1fn).view(np.uint8) & 0xF
        words = c[..., 0::2] | (c[..., 1::2] << 4)
    return np.ascontiguousarray(words), np.ascontiguousarray(byte.astype(np.uint8).reshape(k // 512, 16, n))


def unpack_weight(words, scales, fmt):
    g, p, n, _ = words.shape
    if fmt == "e4m3":
        vals = np.ascontiguousarray(words).view(ml_dtypes.float8_e4m3fn).astype(np.float64)
    else:
        nib = np.empty((g, p, n, 4), np.uint8)
        nib[..., 0::2] = words & 0xF
        nib[..., 1::2] = words >> 4
        vals = E2M1[nib]
    vals = vals * np.repeat(np.exp2(scales.astype(np.float64) - 127.0), 8, axis=1)[..., None]
    return vals.transpose(0, 1, 3, 2).reshape(g * 512, n)

def pack4(w):
    words, scales = pack_weight(w, "e2m1")
    return words.reshape(words.shape[0], 128, -1), scales


def unpack4(words, scales):
    return unpack_weight(words.reshape(words.shape[0], 128, -1, 2), scales, "e2m1")


N, P, D, E, F = 1024, 3, 512, 1024, 1024


def setup_inputs():
    s = mx_kscale(D)
    x = np.random.standard_normal((N, P, D)) + 0.5 * np.random.standard_normal((1, P, D))
    w1a_words, w1a_scales = pack4(np.random.standard_normal((D, E)) / np.sqrt(D) / s[:, None])
    w2a_words, w2a_scales = pack4(np.random.standard_normal((D, E)) / np.sqrt(D) / s[:, None])
    return {"x": bf(x * s),
            "w1a_words": w1a_words, "w1a_scales": w1a_scales,
            "w2a_words": w2a_words, "w2a_scales": w2a_scales}


def reference(x, w1a_words, w1a_scales, w2a_words, w2a_scales):
    h = f64(x)
    neigh = (h.sum(axis=1, keepdims=True) - h) * 0.5
    return (mxq(h, 2, "e4m3") @ unpack4(w2a_words, w2a_scales)) + (mxq(neigh, 2, "e4m3") @ unpack4(w1a_words, w1a_scales))

@@ -1,0 +1,167 @@
+from contextlib import ExitStack
+
+import concourse.masks as masks
+import concourse.mybir as mybir
+
+F32 = mybir.dt.float32
+BF16 = mybir.dt.bfloat16
+I32 = mybir.dt.int32
+U32 = mybir.dt.uint32
+U8 = mybir.dt.uint8
+FP8X4 = mybir.dt.float8_e4m3fn_x4
+FP4X4 = mybir.dt.float4_e2m1fn_x4
+MULT = mybir.AluOpType.mult
+ADD = mybir.AluOpType.add
+
+P = 128
+ITEMS, HOPS, K, E = 1024, 3, 512, 1024
+ROUNDS = ITEMS // P
+PAIRS = K // 2
+N_TILE = 512
+N_TILES = E // N_TILE
+UNITS = 2 * HOPS
+FIRST_UNITS = 4
+HOPS_PER_BANK = 2
+SCALE_ROWS = 4
+
+FLOPS = 2 * 2 * ITEMS * HOPS * K * E
+
+
+def tile_dogtaitujuanji_pa_kernel(
+    tc, x, w1a_words, w1a_scales, w2a_words, w2a_scales, out
+):
+    nc = tc.nc
+    given_words = [w2a_words, w1a_words]
+    given_scales = [w2a_scales, w1a_scales]
+
+    with ExitStack() as ctx:
+        ctx.enter_context(tc.manual_schedule())
+        keep = ctx.enter_context(tc.tile_pool(name="keep", bufs=1))
+        x_pool = ctx.enter_context(tc.tile_pool(name="x_pool", bufs=ROUNDS))
+        prep = ctx.enter_context(tc.tile_pool(name="prep", bufs=2))
+        results = ctx.enter_context(tc.tile_pool(name="results", bufs=3))
+        psum_t = ctx.enter_context(tc.psum_pool(name="psum_t", bufs=1))
+        psum_o = ctx.enter_context(tc.psum_pool(name="psum_o", bufs=6))
+
+        identity = keep.tile([P, P], F32)
+        masks.make_identity(nc, identity[:])
+
+        w_words = keep.tile([P, 2, 2 * E], U8, align_bytes=64)
+        w_planes = keep.tile([P, 2, E], U8, align_bytes=64)
+        nc.vector.memset(w_planes[:].bitcast(I32), 0)
+
+        x_tiles = []
+        for r in range(ROUNDS):
+            x_tile = x_pool.tile([P, HOPS * K], BF16)
+            x_tiles.append(x_tile)
+
+        def load_x(r):
+            nc.sync.dma_start(
+                out=x_tiles[r][:],
+                in_=x[r * P : (r + 1) * P, :, :].rearrange("n h k -> n (h k)"),
+            )
+
+        load_x(0)
+        for operand in range(2):
+            nc.sync.dma_start(
+                out=w_words[:, operand, :].bitcast(I32),
+                in_=given_words[operand][0, :, :].bitcast(I32),
+            )
+        for operand in range(2):
+            for quadrant in range(P // 32):
+                nc.sync.dma_start(
+                    out=w_planes[
+                        32 * quadrant : 32 * quadrant + SCALE_ROWS, operand, :
+                    ].bitcast(I32),
+                    in_=given_scales[operand][
+                        0, SCALE_ROWS * quadrant : SCALE_ROWS * (quadrant + 1), :
+                    ].bitcast(I32),
+                )
+        for r in range(1, ROUNDS):
+            load_x(r)
+
+        def transpose_round(r):
+            words = x_tiles[r][:].bitcast(F32)
+            banks = []
+            for first_hop in range(0, HOPS, HOPS_PER_BANK):
+                bank = psum_t.tile(
+                    [P, HOPS_PER_BANK, 2, P], F32, name="bank%d" % first_hop
+                )
+                for hop in range(first_hop, min(first_hop + HOPS_PER_BANK, HOPS)):
+                    for u in range(2):
+                        nc.tensor.transpose(
+                            bank[:, hop - first_hop, u, :],
+                            words[:, hop * PAIRS + u : (hop + 1) * PAIRS : 2],
+                            identity[:],
+                        )
+                banks.append(bank)
+            return banks
+
+        def quantise(grouped, codes, planes, units):
+            nc.vector.quantize_mx(
+                out=codes[:, units, :].rearrange("p a i -> p (a i)").bitcast(FP8X4),
+                scales=planes[:, units, :].rearrange("p a i -> p (a i)"),
+                in_=grouped[:, units, :].rearrange("p a c -> p (a c)"),
+            )
+
+        def prepare_round(banks):
+            grouped = prep.tile([P, UNITS, P * 4], BF16, align_bytes=64)
+            for b, bank in enumerate(banks):
+                first_hop = b * HOPS_PER_BANK
+                hops_here = min(HOPS_PER_BANK, HOPS - first_hop)
+                nc.vector.tensor_copy(
+                    out=grouped[:, first_hop : first_hop + hops_here, :]
+                    .bitcast(F32)
+                    .rearrange("p h (i u) -> p h i u", u=2),
+                    in_=bank[:, 0:hops_here, :, :].rearrange("p h u i -> p h i u"),
+                )
+            halved = prep.tile([P, HOPS, P * 4], BF16)
+            nc.vector.tensor_scalar(
+                out=halved[:], in0=grouped[:, 0:HOPS, :], scalar1=0.5, scalar2=None, op0=MULT
+            )
+
+            def add_neigh(hop):
+                nc.vector.tensor_tensor(
+                    out=grouped[:, HOPS + hop, :],
+                    in0=halved[:, (hop + 1) % HOPS, :],
+                    in1=halved[:, (hop + 2) % HOPS, :],
+                    op=ADD,
+                )
+
+            codes = prep.tile([P, UNITS, P], U32, align_bytes=64)
+            planes = prep.tile([P, UNITS, P], U8, align_bytes=64)
+            add_neigh(0)
+            add_neigh(1)
+            quantise(grouped, codes, planes, slice(0, FIRST_UNITS))
+            add_neigh(2)
+            quantise(grouped, codes, planes, slice(FIRST_UNITS, UNITS))
+            return codes, planes
+
+        def multiply_round(r, codes, planes):
+            result = results.tile([P, HOPS, E], F32)
+            for hop in range(HOPS):
+                for n in range(N_TILES):
+                    acc = psum_o.tile([P, N_TILE], F32)
+                    for operand in range(2):
+                        unit = operand * HOPS + hop
+                        nc.tensor.matmul_mx(
+                            out=acc[:],
+                            lhsT=codes[:, unit, :].bitcast(FP8X4),
+                            lhsT_scale=planes[:, unit, :],
+                            rhs=w_words[
+                                :, operand, 2 * N_TILE * n : 2 * N_TILE * (n + 1)
+                            ].bitcast(FP4X4),
+                            rhs_scale=w_planes[:, operand, N_TILE * n : N_TILE * (n + 1)],
+                            start=(operand == 0),
+                            stop=(operand == 1),
+                        )
+                    nc.scalar.copy(out=result[:, hop, N_TILE * n : N_TILE * (n + 1)], in_=acc[:])
+                nc.sync.dma_start(out=out[r * P : (r + 1) * P, hop, :], in_=result[:, hop, :])
+
+        ready = prepare_round(transpose_round(0))
+        for r in range(ROUNDS):
+            following = None
+            if r + 1 < ROUNDS:
+                following = prepare_round(transpose_round(r + 1))
+            multiply_round(r, ready[0], ready[1])
+            ready = following

@@ -23,6 +23,7 @@ UNITS = 2 * HOPS
 FIRST_UNITS = 4
 HOPS_PER_BANK = 2
 SCALE_ROWS = 4
+RUN = 2
 
 FLOPS = 2 * 2 * ITEMS * HOPS * K * E
 
@@ -39,9 +40,10 @@ def tile_dogtaitujuanji_pa_kernel(
         keep = ctx.enter_context(tc.tile_pool(name="keep", bufs=1))
         x_pool = ctx.enter_context(tc.tile_pool(name="x_pool", bufs=ROUNDS))
         prep = ctx.enter_context(tc.tile_pool(name="prep", bufs=2))
+        quantised = ctx.enter_context(tc.tile_pool(name="quantised", bufs=RUN + 1))
         results = ctx.enter_context(tc.tile_pool(name="results", bufs=3))
-        psum_t = ctx.enter_context(tc.psum_pool(name="psum_t", bufs=1))
-        psum_o = ctx.enter_context(tc.psum_pool(name="psum_o", bufs=6))
+        psum_t = ctx.enter_context(tc.psum_pool(name="psum_t", bufs=RUN))
+        psum_o = ctx.enter_context(tc.psum_pool(name="psum_o", bufs=8 - 2 * RUN))
 
         identity = keep.tile([P, P], F32)
         masks.make_identity(nc, identity[:])
@@ -55,13 +57,17 @@ def tile_dogtaitujuanji_pa_kernel(
             x_tile = x_pool.tile([P, HOPS * K], BF16)
             x_tiles.append(x_tile)
 
-        def load_x(r):
+        def load_x(r, first_hop, hops):
             nc.sync.dma_start(
-                out=x_tiles[r][:],
-                in_=x[r * P : (r + 1) * P, :, :].rearrange("n h k -> n (h k)"),
+                out=x_tiles[r][:, first_hop * K : (first_hop + hops) * K],
+                in_=x[r * P : (r + 1) * P, first_hop : first_hop + hops, :].rearrange(
+                    "n h k -> n (h k)"
+                ),
             )
 
-        load_x(0)
+        for hop in range(HOPS):
+            load_x(0, hop, 1)
+        load_x(1, 0, HOPS)
         for operand in range(2):
             nc.sync.dma_start(
                 out=w_words[:, operand, :].bitcast(I32),
@@ -77,8 +83,8 @@ def tile_dogtaitujuanji_pa_kernel(
                         0, SCALE_ROWS * quadrant : SCALE_ROWS * (quadrant + 1), :
                     ].bitcast(I32),
                 )
-        for r in range(1, ROUNDS):
-            load_x(r)
+        for r in range(2, ROUNDS):
+            load_x(r, 0, HOPS)
 
         def transpose_round(r):
             words = x_tiles[r][:].bitcast(F32)
@@ -128,8 +134,8 @@ def tile_dogtaitujuanji_pa_kernel(
                     op=ADD,
                 )
 
-            codes = prep.tile([P, UNITS, P], U32, align_bytes=64)
-            planes = prep.tile([P, UNITS, P], U8, align_bytes=64)
+            codes = quantised.tile([P, UNITS, P], U32, align_bytes=64)
+            planes = quantised.tile([P, UNITS, P], U8, align_bytes=64)
             add_neigh(0)
             add_neigh(1)
             quantise(grouped, codes, planes, slice(0, FIRST_UNITS))
@@ -138,9 +144,12 @@ def tile_dogtaitujuanji_pa_kernel(
             return codes, planes
 
         def multiply_round(r, codes, planes):
+            items = slice(r * P, (r + 1) * P)
+            last_round = r == ROUNDS - 1
             result = results.tile([P, HOPS, E], F32)
             for hop in range(HOPS):
                 for n in range(N_TILES):
+                    cols = slice(N_TILE * n, N_TILE * (n + 1))
                     acc = psum_o.tile([P, N_TILE], F32)
                     for operand in range(2):
                         unit = operand * HOPS + hop
@@ -151,17 +160,29 @@ def tile_dogtaitujuanji_pa_kernel(
                             rhs=w_words[
                                 :, operand, 2 * N_TILE * n : 2 * N_TILE * (n + 1)
                             ].bitcast(FP4X4),
-                            rhs_scale=w_planes[:, operand, N_TILE * n : N_TILE * (n + 1)],
+                            rhs_scale=w_planes[:, operand, cols],
                             start=(operand == 0),
                             stop=(operand == 1),
                         )
-                    nc.scalar.copy(out=result[:, hop, N_TILE * n : N_TILE * (n + 1)], in_=acc[:])
-                nc.sync.dma_start(out=out[r * P : (r + 1) * P, hop, :], in_=result[:, hop, :])
+                    if last_round and n % 2 == 1:
+                        nc.vector.tensor_copy(out=result[:, hop, cols], in_=acc[:])
+                    else:
+                        nc.scalar.copy(out=result[:, hop, cols], in_=acc[:])
+                    if last_round:
+                        nc.sync.dma_start(out=out[items, hop, cols], in_=result[:, hop, cols])
+                if not last_round:
+                    nc.sync.dma_start(out=out[items, hop, :], in_=result[:, hop, :])
 
-        ready = prepare_round(transpose_round(0))
+        ready = {}
+
+        def prepare_rounds(first_round):
+            rounds = range(first_round, min(first_round + RUN, ROUNDS))
+            banks = [transpose_round(r) for r in rounds]
+            for r in rounds:
+                ready[r] = prepare_round(banks[r - first_round])
+
+        prepare_rounds(0)
         for r in range(ROUNDS):
-            following = None
-            if r + 1 < ROUNDS:
-                following = prepare_round(transpose_round(r + 1))
-            multiply_round(r, ready[0], ready[1])
-            ready = following
+            multiply_round(r, ready[r][0], ready[r][1])
+            if r % RUN == 0:
+                prepare_rounds(r + RUN)

@@ -20,7 +20,7 @@ PAIRS = K // 2
 N_TILE = 512
 N_TILES = E // N_TILE
 UNITS = 2 * HOPS
-FIRST_UNITS = 4
+UNITS_PER_CALL = 2
 HOPS_PER_BANK = 2
 SCALE_ROWS = 4
 RUN = 2
@@ -39,6 +39,7 @@ def tile_dogtaitujuanji_pa_kernel(
         ctx.enter_context(tc.manual_schedule())
         keep = ctx.enter_context(tc.tile_pool(name="keep", bufs=1))
         x_pool = ctx.enter_context(tc.tile_pool(name="x_pool", bufs=ROUNDS))
+        sorting = ctx.enter_context(tc.tile_pool(name="sorting", bufs=RUN))
         prep = ctx.enter_context(tc.tile_pool(name="prep", bufs=2))
         quantised = ctx.enter_context(tc.tile_pool(name="quantised", bufs=RUN + 1))
         results = ctx.enter_context(tc.tile_pool(name="results", bufs=3))
@@ -86,8 +87,22 @@ def tile_dogtaitujuanji_pa_kernel(
         for r in range(2, ROUNDS):
             load_x(r, 0, HOPS)
 
+        sorted_tiles = {}
+
+        def sort_words(r):
+            sorted_words = sorting.tile([P, HOPS, 2, P], F32)
+            nc.vector.tensor_copy(
+                out=sorted_words[:],
+                in_=x_tiles[r][:].bitcast(F32).rearrange("n (h p u) -> n h u p", h=HOPS, u=2),
+            )
+            sorted_tiles[r] = sorted_words
+
+        def words_to_transpose(r, hop, u):
+            if r in sorted_tiles:
+                return sorted_tiles[r][:, hop, u, :]
+            return x_tiles[r][:].bitcast(F32)[:, hop * PAIRS + u : (hop + 1) * PAIRS : 2]
+
         def transpose_round(r):
-            words = x_tiles[r][:].bitcast(F32)
             banks = []
             for first_hop in range(0, HOPS, HOPS_PER_BANK):
                 bank = psum_t.tile(
@@ -96,14 +111,13 @@ def tile_dogtaitujuanji_pa_kernel(
                 for hop in range(first_hop, min(first_hop + HOPS_PER_BANK, HOPS)):
                     for u in range(2):
                         nc.tensor.transpose(
-                            bank[:, hop - first_hop, u, :],
-                            words[:, hop * PAIRS + u : (hop + 1) * PAIRS : 2],
-                            identity[:],
+                            bank[:, hop - first_hop, u, :], words_to_transpose(r, hop, u), identity[:]
                         )
                 banks.append(bank)
             return banks
 
-        def quantise(grouped, codes, planes, units):
+        def quantise(grouped, codes, planes, call):
+            units = slice(call * UNITS_PER_CALL, (call + 1) * UNITS_PER_CALL)
             nc.vector.quantize_mx(
                 out=codes[:, units, :].rearrange("p a i -> p (a i)").bitcast(FP8X4),
                 scales=planes[:, units, :].rearrange("p a i -> p (a i)"),
@@ -121,6 +135,9 @@ def tile_dogtaitujuanji_pa_kernel(
                     .rearrange("p h (i u) -> p h i u", u=2),
                     in_=bank[:, 0:hops_here, :, :].rearrange("p h u i -> p h i u"),
                 )
+            codes = quantised.tile([P, UNITS, P], U32, align_bytes=64)
+            planes = quantised.tile([P, UNITS, P], U8, align_bytes=64)
+            quantise(grouped, codes, planes, 0)
             halved = prep.tile([P, HOPS, P * 4], BF16)
             nc.vector.tensor_scalar(
                 out=halved[:], in0=grouped[:, 0:HOPS, :], scalar1=0.5, scalar2=None, op0=MULT
@@ -134,13 +151,11 @@ def tile_dogtaitujuanji_pa_kernel(
                     op=ADD,
                 )
 
-            codes = quantised.tile([P, UNITS, P], U32, align_bytes=64)
-            planes = quantised.tile([P, UNITS, P], U8, align_bytes=64)
             add_neigh(0)
             add_neigh(1)
-            quantise(grouped, codes, planes, slice(0, FIRST_UNITS))
+            quantise(grouped, codes, planes, 1)
             add_neigh(2)
-            quantise(grouped, codes, planes, slice(FIRST_UNITS, UNITS))
+            quantise(grouped, codes, planes, 2)
             return codes, planes
 
         def multiply_round(r, codes, planes):
@@ -148,26 +163,27 @@ def tile_dogtaitujuanji_pa_kernel(
             last_round = r == ROUNDS - 1
             result = results.tile([P, HOPS, E], F32)
             for hop in range(HOPS):
-                for n in range(N_TILES):
-                    cols = slice(N_TILE * n, N_TILE * (n + 1))
-                    acc = psum_o.tile([P, N_TILE], F32)
-                    for operand in range(2):
-                        unit = operand * HOPS + hop
+                accs = [psum_o.tile([P, N_TILE], F32, name="acc") for n in range(N_TILES)]
+                for operand in range(2):
+                    unit = operand * HOPS + hop
+                    for n in range(N_TILES):
                         nc.tensor.matmul_mx(
-                            out=acc[:],
+                            out=accs[n][:],
                             lhsT=codes[:, unit, :].bitcast(FP8X4),
                             lhsT_scale=planes[:, unit, :],
                             rhs=w_words[
                                 :, operand, 2 * N_TILE * n : 2 * N_TILE * (n + 1)
                             ].bitcast(FP4X4),
-                            rhs_scale=w_planes[:, operand, cols],
+                            rhs_scale=w_planes[:, operand, N_TILE * n : N_TILE * (n + 1)],
                             start=(operand == 0),
                             stop=(operand == 1),
                         )
+                for n in range(N_TILES):
+                    cols = slice(N_TILE * n, N_TILE * (n + 1))
                     if last_round and n % 2 == 1:
-                        nc.vector.tensor_copy(out=result[:, hop, cols], in_=acc[:])
+                        nc.vector.tensor_copy(out=result[:, hop, cols], in_=accs[n][:])
                     else:
-                        nc.scalar.copy(out=result[:, hop, cols], in_=acc[:])
+                        nc.scalar.copy(out=result[:, hop, cols], in_=accs[n][:])
                     if last_round:
                         nc.sync.dma_start(out=out[items, hop, cols], in_=result[:, hop, cols])
                 if not last_round:
@@ -180,6 +196,8 @@ def tile_dogtaitujuanji_pa_kernel(
             banks = [transpose_round(r) for r in rounds]
             for r in rounds:
                 ready[r] = prepare_round(banks[r - first_round])
+            for r in range(first_round + RUN, min(first_round + 2 * RUN, ROUNDS)):
+                sort_words(r)
 
         prepare_rounds(0)
         for r in range(ROUNDS):

@@ -39,7 +39,6 @@ def tile_dogtaitujuanji_pa_kernel(
         ctx.enter_context(tc.manual_schedule())
         keep = ctx.enter_context(tc.tile_pool(name="keep", bufs=1))
         x_pool = ctx.enter_context(tc.tile_pool(name="x_pool", bufs=ROUNDS))
-        sorting = ctx.enter_context(tc.tile_pool(name="sorting", bufs=RUN))
         prep = ctx.enter_context(tc.tile_pool(name="prep", bufs=2))
         quantised = ctx.enter_context(tc.tile_pool(name="quantised", bufs=RUN + 1))
         results = ctx.enter_context(tc.tile_pool(name="results", bufs=3))
@@ -70,11 +69,6 @@ def tile_dogtaitujuanji_pa_kernel(
             load_x(0, hop, 1)
         load_x(1, 0, HOPS)
         for operand in range(2):
-            nc.sync.dma_start(
-                out=w_words[:, operand, :].bitcast(I32),
-                in_=given_words[operand][0, :, :].bitcast(I32),
-            )
-        for operand in range(2):
             for quadrant in range(P // 32):
                 nc.sync.dma_start(
                     out=w_planes[
@@ -84,25 +78,15 @@ def tile_dogtaitujuanji_pa_kernel(
                         0, SCALE_ROWS * quadrant : SCALE_ROWS * (quadrant + 1), :
                     ].bitcast(I32),
                 )
+            nc.sync.dma_start(
+                out=w_words[:, operand, :].bitcast(I32),
+                in_=given_words[operand][0, :, :].bitcast(I32),
+            )
         for r in range(2, ROUNDS):
             load_x(r, 0, HOPS)
 
-        sorted_tiles = {}
-
-        def sort_words(r):
-            sorted_words = sorting.tile([P, HOPS, 2, P], F32)
-            nc.vector.tensor_copy(
-                out=sorted_words[:],
-                in_=x_tiles[r][:].bitcast(F32).rearrange("n (h p u) -> n h u p", h=HOPS, u=2),
-            )
-            sorted_tiles[r] = sorted_words
-
-        def words_to_transpose(r, hop, u):
-            if r in sorted_tiles:
-                return sorted_tiles[r][:, hop, u, :]
-            return x_tiles[r][:].bitcast(F32)[:, hop * PAIRS + u : (hop + 1) * PAIRS : 2]
-
         def transpose_round(r):
+            words = x_tiles[r][:].bitcast(F32)
             banks = []
             for first_hop in range(0, HOPS, HOPS_PER_BANK):
                 bank = psum_t.tile(
@@ -111,7 +95,9 @@ def tile_dogtaitujuanji_pa_kernel(
                 for hop in range(first_hop, min(first_hop + HOPS_PER_BANK, HOPS)):
                     for u in range(2):
                         nc.tensor.transpose(
-                            bank[:, hop - first_hop, u, :], words_to_transpose(r, hop, u), identity[:]
+                            bank[:, hop - first_hop, u, :],
+                            words[:, hop * PAIRS + u : (hop + 1) * PAIRS : 2],
+                            identity[:],
                         )
                 banks.append(bank)
             return banks
@@ -139,22 +125,18 @@ def tile_dogtaitujuanji_pa_kernel(
             planes = quantised.tile([P, UNITS, P], U8, align_bytes=64)
             quantise(grouped, codes, planes, 0)
             halved = prep.tile([P, HOPS, P * 4], BF16)
-            nc.vector.tensor_scalar(
-                out=halved[:], in0=grouped[:, 0:HOPS, :], scalar1=0.5, scalar2=None, op0=MULT
-            )
-
-            def add_neigh(hop):
+            for hops in (slice(1, HOPS), slice(0, 1)):
+                nc.vector.tensor_scalar(
+                    out=halved[:, hops, :], in0=grouped[:, hops, :], scalar1=0.5, scalar2=None, op0=MULT
+                )
+            for hop in range(HOPS):
                 nc.vector.tensor_tensor(
                     out=grouped[:, HOPS + hop, :],
                     in0=halved[:, (hop + 1) % HOPS, :],
                     in1=halved[:, (hop + 2) % HOPS, :],
                     op=ADD,
                 )
-
-            add_neigh(0)
-            add_neigh(1)
             quantise(grouped, codes, planes, 1)
-            add_neigh(2)
             quantise(grouped, codes, planes, 2)
             return codes, planes
 
@@ -196,8 +178,6 @@ def tile_dogtaitujuanji_pa_kernel(
             banks = [transpose_round(r) for r in rounds]
             for r in rounds:
                 ready[r] = prepare_round(banks[r - first_round])
-            for r in range(first_round + RUN, min(first_round + 2 * RUN, ROUNDS)):
-                sort_words(r)
 
         prepare_rounds(0)
         for r in range(ROUNDS):

@@ -166,9 +166,9 @@ def tile_dogtaitujuanji_pa_kernel(
                         nc.vector.tensor_copy(out=result[:, hop, cols], in_=accs[n][:])
                     else:
                         nc.scalar.copy(out=result[:, hop, cols], in_=accs[n][:])
-                    if last_round:
+                    if last_round and hop == HOPS - 1:
                         nc.sync.dma_start(out=out[items, hop, cols], in_=result[:, hop, cols])
-                if not last_round:
+                if not (last_round and hop == HOPS - 1):
                     nc.sync.dma_start(out=out[items, hop, :], in_=result[:, hop, :])
 
         ready = {}

@@ -40,6 +40,7 @@ def tile_dogtaitujuanji_pa_kernel(
         keep = ctx.enter_context(tc.tile_pool(name="keep", bufs=1))
         x_pool = ctx.enter_context(tc.tile_pool(name="x_pool", bufs=ROUNDS))
         prep = ctx.enter_context(tc.tile_pool(name="prep", bufs=2))
+        sort_pool = ctx.enter_context(tc.tile_pool(name="sort_pool", bufs=2 * RUN))
         quantised = ctx.enter_context(tc.tile_pool(name="quantised", bufs=RUN + 1))
         results = ctx.enter_context(tc.tile_pool(name="results", bufs=3))
         psum_t = ctx.enter_context(tc.psum_pool(name="psum_t", bufs=RUN))
@@ -85,6 +86,16 @@ def tile_dogtaitujuanji_pa_kernel(
         for r in range(2, ROUNDS):
             load_x(r, 0, HOPS)
 
+        sorted_words = {}
+
+        def sort_round(r):
+            tile = sort_pool.tile([P, HOPS * PAIRS], F32, name="sorted")
+            nc.vector.tensor_copy(
+                out=tile[:].rearrange("n (h u p) -> n u h p", h=HOPS, u=2),
+                in_=x_tiles[r][:].bitcast(F32).rearrange("n (h p u) -> n u h p", h=HOPS, u=2),
+            )
+            sorted_words[r] = tile
+
         def transpose_round(r):
             words = x_tiles[r][:].bitcast(F32)
             banks = []
@@ -94,11 +105,12 @@ def tile_dogtaitujuanji_pa_kernel(
                 )
                 for hop in range(first_hop, min(first_hop + HOPS_PER_BANK, HOPS)):
                     for u in range(2):
-                        nc.tensor.transpose(
-                            bank[:, hop - first_hop, u, :],
-                            words[:, hop * PAIRS + u : (hop + 1) * PAIRS : 2],
-                            identity[:],
-                        )
+                        if r in sorted_words:
+                            start = hop * PAIRS + u * P
+                            in_words = sorted_words[r][:, start : start + P]
+                        else:
+                            in_words = words[:, hop * PAIRS + u : (hop + 1) * PAIRS : 2]
+                        nc.tensor.transpose(bank[:, hop - first_hop, u, :], in_words, identity[:])
                 banks.append(bank)
             return banks
 
@@ -176,6 +188,9 @@ def tile_dogtaitujuanji_pa_kernel(
         def prepare_rounds(first_round):
             rounds = range(first_round, min(first_round + RUN, ROUNDS))
             banks = [transpose_round(r) for r in rounds]
+            if first_round > 0:
+                for r in range(first_round + RUN, min(first_round + 2 * RUN, ROUNDS)):
+                    sort_round(r)
             for r in rounds:
                 ready[r] = prepare_round(banks[r - first_round])
 

@@ -20,6 +20,8 @@ PAIRS = K // 2
 N_TILE = 512
 N_TILES = E // N_TILE
 UNITS = 2 * HOPS
+X_UNITS = (2, 3, 4)
+NEIGH_UNITS = (1, 5, 0)
 UNITS_PER_CALL = 2
 HOPS_PER_BANK = 2
 SCALE_ROWS = 4
@@ -114,42 +116,51 @@ def tile_dogtaitujuanji_pa_kernel(
                 banks.append(bank)
             return banks
 
-        def quantise(grouped, codes, planes, call):
-            units = slice(call * UNITS_PER_CALL, (call + 1) * UNITS_PER_CALL)
+        def quantise(grouped, codes, planes, first_unit):
+            units = slice(first_unit, first_unit + UNITS_PER_CALL)
             nc.vector.quantize_mx(
                 out=codes[:, units, :].rearrange("p a i -> p (a i)").bitcast(FP8X4),
                 scales=planes[:, units, :].rearrange("p a i -> p (a i)"),
                 in_=grouped[:, units, :].rearrange("p a c -> p (a c)"),
             )
 
-        def prepare_round(banks):
+        def prepare_round(banks, sort_next):
             grouped = prep.tile([P, UNITS, P * 4], BF16, align_bytes=64)
             for b, bank in enumerate(banks):
                 first_hop = b * HOPS_PER_BANK
                 hops_here = min(HOPS_PER_BANK, HOPS - first_hop)
+                first_unit = X_UNITS[first_hop]
                 nc.vector.tensor_copy(
-                    out=grouped[:, first_hop : first_hop + hops_here, :]
+                    out=grouped[:, first_unit : first_unit + hops_here, :]
                     .bitcast(F32)
                     .rearrange("p h (i u) -> p h i u", u=2),
                     in_=bank[:, 0:hops_here, :, :].rearrange("p h u i -> p h i u"),
                 )
             codes = quantised.tile([P, UNITS, P], U32, align_bytes=64)
             planes = quantised.tile([P, UNITS, P], U8, align_bytes=64)
-            quantise(grouped, codes, planes, 0)
             halved = prep.tile([P, HOPS, P * 4], BF16)
-            for hops in (slice(1, HOPS), slice(0, 1)):
+            if sort_next is not None:
+                sort_round(sort_next)
+                halvings = [slice(0, HOPS)]
+            else:
+                halvings = [slice(0, 2), slice(2, HOPS)]
+            x_of_all = grouped[:, X_UNITS[0] : X_UNITS[0] + HOPS, :]
+            for hops in halvings:
                 nc.vector.tensor_scalar(
-                    out=halved[:, hops, :], in0=grouped[:, hops, :], scalar1=0.5, scalar2=None, op0=MULT
+                    out=halved[:, hops, :], in0=x_of_all[:, hops, :], scalar1=0.5, scalar2=None, op0=MULT
                 )
-            for hop in range(HOPS):
-                nc.vector.tensor_tensor(
-                    out=grouped[:, HOPS + hop, :],
-                    in0=halved[:, (hop + 1) % HOPS, :],
-                    in1=halved[:, (hop + 2) % HOPS, :],
-                    op=ADD,
-                )
-            quantise(grouped, codes, planes, 1)
-            quantise(grouped, codes, planes, 2)
+            quantise(grouped, codes, planes, X_UNITS[0])
+            nc.vector.tensor_tensor(
+                out=grouped[:, NEIGH_UNITS[2] : NEIGH_UNITS[2] + 2, :],
+                in0=halved[:, 0:2, :],
+                in1=halved[:, 1:3, :],
+                op=ADD,
+            )
+            nc.vector.tensor_tensor(
+                out=grouped[:, NEIGH_UNITS[1], :], in0=halved[:, 0, :], in1=halved[:, 2, :], op=ADD
+            )
+            quantise(grouped, codes, planes, NEIGH_UNITS[2])
+            quantise(grouped, codes, planes, X_UNITS[2])
             return codes, planes
 
         def multiply_round(r, codes, planes):
@@ -159,7 +170,7 @@ def tile_dogtaitujuanji_pa_kernel(
             for hop in range(HOPS):
                 accs = [psum_o.tile([P, N_TILE], F32, name="acc") for n in range(N_TILES)]
                 for operand in range(2):
-                    unit = operand * HOPS + hop
+                    unit = (X_UNITS, NEIGH_UNITS)[operand][hop]
                     for n in range(N_TILES):
                         nc.tensor.matmul_mx(
                             out=accs[n][:],
@@ -188,11 +199,9 @@ def tile_dogtaitujuanji_pa_kernel(
         def prepare_rounds(first_round):
             rounds = range(first_round, min(first_round + RUN, ROUNDS))
             banks = [transpose_round(r) for r in rounds]
-            if first_round > 0:
-                for r in range(first_round + RUN, min(first_round + 2 * RUN, ROUNDS)):
-                    sort_round(r)
             for r in rounds:
-                ready[r] = prepare_round(banks[r - first_round])
+                sort_next = r + RUN if 0 < first_round and r + RUN < ROUNDS else None
+                ready[r] = prepare_round(banks[r - first_round], sort_next)
 
         prepare_rounds(0)
         for r in range(ROUNDS):

@@ -45,8 +45,8 @@ def tile_dogtaitujuanji_pa_kernel(
         sort_pool = ctx.enter_context(tc.tile_pool(name="sort_pool", bufs=2 * RUN))
         quantised = ctx.enter_context(tc.tile_pool(name="quantised", bufs=RUN + 1))
         results = ctx.enter_context(tc.tile_pool(name="results", bufs=3))
-        psum_t = ctx.enter_context(tc.psum_pool(name="psum_t", bufs=RUN))
-        psum_o = ctx.enter_context(tc.psum_pool(name="psum_o", bufs=8 - 2 * RUN))
+        psum_t = ctx.enter_context(tc.psum_pool(name="psum_t", bufs=1))
+        psum_o = ctx.enter_context(tc.psum_pool(name="psum_o", bufs=5))
 
         identity = keep.tile([P, P], F32)
         masks.make_identity(nc, identity[:])
@@ -98,23 +98,34 @@ def tile_dogtaitujuanji_pa_kernel(
             )
             sorted_words[r] = tile
 
-        def transpose_round(r):
+        def transpose_hop(r, hop, bank):
             words = x_tiles[r][:].bitcast(F32)
-            banks = []
-            for first_hop in range(0, HOPS, HOPS_PER_BANK):
-                bank = psum_t.tile(
-                    [P, HOPS_PER_BANK, 2, P], F32, name="bank%d" % first_hop
-                )
-                for hop in range(first_hop, min(first_hop + HOPS_PER_BANK, HOPS)):
-                    for u in range(2):
-                        if r in sorted_words:
-                            start = hop * PAIRS + u * P
-                            in_words = sorted_words[r][:, start : start + P]
-                        else:
-                            in_words = words[:, hop * PAIRS + u : (hop + 1) * PAIRS : 2]
-                        nc.tensor.transpose(bank[:, hop - first_hop, u, :], in_words, identity[:])
-                banks.append(bank)
-            return banks
+            for u in range(2):
+                if r in sorted_words:
+                    start = hop * PAIRS + u * P
+                    in_words = sorted_words[r][:, start : start + P]
+                else:
+                    in_words = words[:, hop * PAIRS + u : (hop + 1) * PAIRS : 2]
+                nc.tensor.transpose(bank[:, u, :], in_words, identity[:])
+
+        def transpose_run(first_round):
+            first = psum_t.tile([P, 2, 2, P], F32, name="bank_first")
+            shared = psum_t.tile([P, 2, 2, P], F32, name="bank_shared")
+            second = psum_t.tile([P, 2, 2, P], F32, name="bank_second")
+            last_hops = [shared, shared]
+            if first_round == 0:
+                own = psum_o.tile([P, 2, 2, P], F32, name="acc")
+                last_hops = [shared, own]
+            for hop in range(2):
+                transpose_hop(first_round, hop, first[:, hop, :, :])
+            for i in range(2):
+                transpose_hop(first_round + i, 2, last_hops[i][:, i, :, :])
+            for hop in range(2):
+                transpose_hop(first_round + 1, hop, second[:, hop, :, :])
+            return [
+                (first[:], last_hops[0][:, 0:1, :, :]),
+                (second[:], last_hops[1][:, 1:2, :, :]),
+            ]
 
         def quantise(grouped, codes, planes, first_unit):
             units = slice(first_unit, first_unit + UNITS_PER_CALL)
@@ -134,13 +145,13 @@ def tile_dogtaitujuanji_pa_kernel(
                     out=grouped[:, first_unit : first_unit + hops_here, :]
                     .bitcast(F32)
                     .rearrange("p h (i u) -> p h i u", u=2),
-                    in_=bank[:, 0:hops_here, :, :].rearrange("p h u i -> p h i u"),
+                    in_=bank.rearrange("p h u i -> p h i u"),
                 )
             codes = quantised.tile([P, UNITS, P], U32, align_bytes=64)
             planes = quantised.tile([P, UNITS, P], U8, align_bytes=64)
             halved = prep.tile([P, HOPS, P * 4], BF16)
-            if sort_next is not None:
-                sort_round(sort_next)
+            if sort_next:
+                sort_round(sort_next[0])
                 halvings = [slice(0, HOPS)]
             else:
                 halvings = [slice(0, 2), slice(2, HOPS)]
@@ -149,6 +160,8 @@ def tile_dogtaitujuanji_pa_kernel(
                 nc.vector.tensor_scalar(
                     out=halved[:, hops, :], in0=x_of_all[:, hops, :], scalar1=0.5, scalar2=None, op0=MULT
                 )
+            for r in sort_next[1:]:
+                sort_round(r)
             quantise(grouped, codes, planes, X_UNITS[0])
             nc.vector.tensor_tensor(
                 out=grouped[:, NEIGH_UNITS[2] : NEIGH_UNITS[2] + 2, :],
@@ -198,9 +211,11 @@ def tile_dogtaitujuanji_pa_kernel(
 
         def prepare_rounds(first_round):
             rounds = range(first_round, min(first_round + RUN, ROUNDS))
-            banks = [transpose_round(r) for r in rounds]
+            if first_round == ROUNDS:
+                return
+            banks = transpose_run(first_round)
             for r in rounds:
-                sort_next = r + RUN if 0 < first_round and r + RUN < ROUNDS else None
+                sort_next = {0: [], 1: [2, 3]}.get(r, [s for s in [r + RUN] if s < ROUNDS])
                 ready[r] = prepare_round(banks[r - first_round], sort_next)
 
         prepare_rounds(0)

@@ -68,10 +68,7 @@ def tile_dogtaitujuanji_pa_kernel(
                 ),
             )
 
-        for hop in range(HOPS):
-            load_x(0, hop, 1)
-        load_x(1, 0, HOPS)
-        for operand in range(2):
+        def load_scales(operand):
             for quadrant in range(P // 32):
                 nc.sync.dma_start(
                     out=w_planes[
@@ -81,10 +78,20 @@ def tile_dogtaitujuanji_pa_kernel(
                         0, SCALE_ROWS * quadrant : SCALE_ROWS * (quadrant + 1), :
                     ].bitcast(I32),
                 )
+
+        def load_words(operand):
             nc.sync.dma_start(
                 out=w_words[:, operand, :].bitcast(I32),
                 in_=given_words[operand][0, :, :].bitcast(I32),
             )
+
+        for hop in range(HOPS):
+            load_x(0, hop, 1)
+        load_x(1, 0, HOPS)
+        load_scales(0)
+        load_words(0)
+        load_words(1)
+        load_scales(1)
         for r in range(2, ROUNDS):
             load_x(r, 0, HOPS)
 
@@ -182,23 +189,26 @@ def tile_dogtaitujuanji_pa_kernel(
             result = results.tile([P, HOPS, E], F32)
             for hop in range(HOPS):
                 accs = [psum_o.tile([P, N_TILE], F32, name="acc") for n in range(N_TILES)]
-                for operand in range(2):
+                if r == 0:
+                    order = [(operand, n) for operand in range(2) for n in range(N_TILES)]
+                else:
+                    order = [(operand, n) for n in range(N_TILES) for operand in range(2)]
+                for operand, n in order:
                     unit = (X_UNITS, NEIGH_UNITS)[operand][hop]
-                    for n in range(N_TILES):
-                        nc.tensor.matmul_mx(
-                            out=accs[n][:],
-                            lhsT=codes[:, unit, :].bitcast(FP8X4),
-                            lhsT_scale=planes[:, unit, :],
-                            rhs=w_words[
-                                :, operand, 2 * N_TILE * n : 2 * N_TILE * (n + 1)
-                            ].bitcast(FP4X4),
-                            rhs_scale=w_planes[:, operand, N_TILE * n : N_TILE * (n + 1)],
-                            start=(operand == 0),
-                            stop=(operand == 1),
-                        )
+                    nc.tensor.matmul_mx(
+                        out=accs[n][:],
+                        lhsT=codes[:, unit, :].bitcast(FP8X4),
+                        lhsT_scale=planes[:, unit, :],
+                        rhs=w_words[
+                            :, operand, 2 * N_TILE * n : 2 * N_TILE * (n + 1)
+                        ].bitcast(FP4X4),
+                        rhs_scale=w_planes[:, operand, N_TILE * n : N_TILE * (n + 1)],
+                        start=(operand == 0),
+                        stop=(operand == 1),
+                    )
                 for n in range(N_TILES):
                     cols = slice(N_TILE * n, N_TILE * (n + 1))
-                    if last_round and n % 2 == 1:
+                    if n % 2 == 1 and (last_round or (r == ROUNDS - 2 and hop == HOPS - 1)):
                         nc.vector.tensor_copy(out=result[:, hop, cols], in_=accs[n][:])
                     else:
                         nc.scalar.copy(out=result[:, hop, cols], in_=accs[n][:])

@@ -51,6 +51,9 @@ def tile_dogtaitujuanji_pa_kernel(
         identity = keep.tile([P, P], F32)
         masks.make_identity(nc, identity[:])
 
+        zeros = keep.tile([P, N_TILE], BF16)
+        nc.vector.memset(zeros[:].bitcast(I32), 0)
+
         w_words = keep.tile([P, 2, 2 * E], U8, align_bytes=64)
         w_planes = keep.tile([P, 2, E], U8, align_bytes=64)
         nc.vector.memset(w_planes[:].bitcast(I32), 0)
@@ -115,6 +118,11 @@ def tile_dogtaitujuanji_pa_kernel(
                     in_words = words[:, hop * PAIRS + u : (hop + 1) * PAIRS : 2]
                 nc.tensor.transpose(bank[:, u, :], in_words, identity[:])
 
+        def warm_up(count):
+            for i in range(count):
+                idle = psum_o.tile([P, N_TILE], F32, name="acc")
+                nc.tensor.matmul(idle[:], lhsT=zeros[:, 0:P], rhs=zeros[:], start=True, stop=True)
+
         def transpose_run(first_round):
             first = psum_t.tile([P, 2, 2, P], F32, name="bank_first")
             shared = psum_t.tile([P, 2, 2, P], F32, name="bank_shared")
@@ -123,9 +131,12 @@ def tile_dogtaitujuanji_pa_kernel(
             if first_round == 0:
                 own = psum_o.tile([P, 2, 2, P], F32, name="acc")
                 last_hops = [shared, own]
+                warm_up(4)
             for hop in range(2):
                 transpose_hop(first_round, hop, first[:, hop, :, :])
             for i in range(2):
+                if first_round + i == 1:
+                    warm_up(2)
                 transpose_hop(first_round + i, 2, last_hops[i][:, i, :, :])
             for hop in range(2):
                 transpose_hop(first_round + 1, hop, second[:, hop, :, :])
@@ -142,13 +153,13 @@ def tile_dogtaitujuanji_pa_kernel(
                 in_=grouped[:, units, :].rearrange("p a c -> p (a c)"),
             )
 
-        def prepare_round(banks, sort_next):
+        def prepare_round(banks, sort_next, copies):
             grouped = prep.tile([P, UNITS, P * 4], BF16, align_bytes=64)
             for b, bank in enumerate(banks):
                 first_hop = b * HOPS_PER_BANK
                 hops_here = min(HOPS_PER_BANK, HOPS - first_hop)
                 first_unit = X_UNITS[first_hop]
-                nc.vector.tensor_copy(
+                copies[b](
                     out=grouped[:, first_unit : first_unit + hops_here, :]
                     .bitcast(F32)
                     .rearrange("p h (i u) -> p h i u", u=2),
@@ -224,9 +235,13 @@ def tile_dogtaitujuanji_pa_kernel(
             if first_round == ROUNDS:
                 return
             banks = transpose_run(first_round)
+            if first_round == 0:
+                warm_up(1)
             for r in rounds:
                 sort_next = {0: [], 1: [2, 3]}.get(r, [s for s in [r + RUN] if s < ROUNDS])
-                ready[r] = prepare_round(banks[r - first_round], sort_next)
+                vector, scalar = nc.vector.tensor_copy, nc.scalar.copy
+                copies = {0: (vector, scalar), 1: (scalar, scalar)}.get(r, (vector, vector))
+                ready[r] = prepare_round(banks[r - first_round], sort_next, copies)
 
         prepare_rounds(0)
         for r in range(ROUNDS):

@@ -153,7 +153,7 @@ def tile_dogtaitujuanji_pa_kernel(
                 in_=grouped[:, units, :].rearrange("p a c -> p (a c)"),
             )
 
-        def prepare_round(banks, sort_next, copies):
+        def prepare_round(banks, copies, sort_between=()):
             grouped = prep.tile([P, UNITS, P * 4], BF16, align_bytes=64)
             for b, bank in enumerate(banks):
                 first_hop = b * HOPS_PER_BANK
@@ -168,25 +168,22 @@ def tile_dogtaitujuanji_pa_kernel(
             codes = quantised.tile([P, UNITS, P], U32, align_bytes=64)
             planes = quantised.tile([P, UNITS, P], U8, align_bytes=64)
             halved = prep.tile([P, HOPS, P * 4], BF16)
-            if sort_next:
-                sort_round(sort_next[0])
-                halvings = [slice(0, HOPS)]
-            else:
-                halvings = [slice(0, 2), slice(2, HOPS)]
             x_of_all = grouped[:, X_UNITS[0] : X_UNITS[0] + HOPS, :]
-            for hops in halvings:
+            for hops in (slice(0, 2), slice(2, HOPS)):
                 nc.vector.tensor_scalar(
                     out=halved[:, hops, :], in0=x_of_all[:, hops, :], scalar1=0.5, scalar2=None, op0=MULT
                 )
-            for r in sort_next[1:]:
-                sort_round(r)
             quantise(grouped, codes, planes, X_UNITS[0])
+            for r in sort_between[:1]:
+                sort_round(r)
             nc.vector.tensor_tensor(
                 out=grouped[:, NEIGH_UNITS[2] : NEIGH_UNITS[2] + 2, :],
                 in0=halved[:, 0:2, :],
                 in1=halved[:, 1:3, :],
                 op=ADD,
             )
+            for r in sort_between[1:]:
+                sort_round(r)
             nc.vector.tensor_tensor(
                 out=grouped[:, NEIGH_UNITS[1], :], in0=halved[:, 0, :], in1=halved[:, 2, :], op=ADD
             )
@@ -229,22 +226,21 @@ def tile_dogtaitujuanji_pa_kernel(
                     nc.sync.dma_start(out=out[items, hop, :], in_=result[:, hop, :])
 
         ready = {}
+        by_vector, by_scalar = nc.vector.tensor_copy, nc.scalar.copy
+
+        banks = transpose_run(0)
+        warm_up(1)
+        ready[0] = prepare_round(banks[0], (by_vector, by_scalar))
+        ready[1] = prepare_round(banks[1], (by_scalar, by_scalar), (2, 3))
 
         def prepare_rounds(first_round):
-            rounds = range(first_round, min(first_round + RUN, ROUNDS))
-            if first_round == ROUNDS:
-                return
             banks = transpose_run(first_round)
-            if first_round == 0:
-                warm_up(1)
-            for r in rounds:
-                sort_next = {0: [], 1: [2, 3]}.get(r, [s for s in [r + RUN] if s < ROUNDS])
-                vector, scalar = nc.vector.tensor_copy, nc.scalar.copy
-                copies = {0: (vector, scalar), 1: (scalar, scalar)}.get(r, (vector, vector))
-                ready[r] = prepare_round(banks[r - first_round], sort_next, copies)
+            ready[first_round] = prepare_round(banks[0], (by_vector, by_vector))
+            for r in range(first_round + RUN, min(first_round + 2 * RUN, ROUNDS)):
+                sort_round(r)
+            ready[first_round + 1] = prepare_round(banks[1], (by_vector, by_vector))
 
-        prepare_rounds(0)
         for r in range(ROUNDS):
             multiply_round(r, ready[r][0], ready[r][1])
-            if r % RUN == 0:
+            if r % RUN == 0 and r + RUN < ROUNDS:
                 prepare_rounds(r + RUN)

from contextlib import ExitStack

import concourse.masks as masks
import concourse.mybir as mybir

F32 = mybir.dt.float32
BF16 = mybir.dt.bfloat16
I32 = mybir.dt.int32
U32 = mybir.dt.uint32
U8 = mybir.dt.uint8
FP8X4 = mybir.dt.float8_e4m3fn_x4
FP4X4 = mybir.dt.float4_e2m1fn_x4
MULT = mybir.AluOpType.mult
ADD = mybir.AluOpType.add

P = 128
ITEMS, HOPS, K, E = 1024, 3, 512, 1024
ROUNDS = ITEMS // P
PAIRS = K // 2
N_TILE = 512
N_TILES = E // N_TILE
UNITS = 2 * HOPS
X_UNITS = (2, 3, 4)
NEIGH_UNITS = (1, 5, 0)
UNITS_PER_CALL = 2
HOPS_PER_BANK = 2
SCALE_ROWS = 4
RUN = 2

FLOPS = 2 * 2 * ITEMS * HOPS * K * E


def tile_dogtaitujuanji_pa_kernel(
    tc, x, w1a_words, w1a_scales, w2a_words, w2a_scales, out
):
    nc = tc.nc
    given_words = [w2a_words, w1a_words]
    given_scales = [w2a_scales, w1a_scales]

    with ExitStack() as ctx:
        ctx.enter_context(tc.manual_schedule())
        keep = ctx.enter_context(tc.tile_pool(name="keep", bufs=1))
        x_pool = ctx.enter_context(tc.tile_pool(name="x_pool", bufs=ROUNDS))
        prep = ctx.enter_context(tc.tile_pool(name="prep", bufs=2))
        sort_pool = ctx.enter_context(tc.tile_pool(name="sort_pool", bufs=2 * RUN))
        quantised = ctx.enter_context(tc.tile_pool(name="quantised", bufs=RUN + 1))
        results = ctx.enter_context(tc.tile_pool(name="results", bufs=3))
        psum_t = ctx.enter_context(tc.psum_pool(name="psum_t", bufs=1))
        psum_o = ctx.enter_context(tc.psum_pool(name="psum_o", bufs=5))

        identity = keep.tile([P, P], F32)
        masks.make_identity(nc, identity[:])

        zeros = keep.tile([P, N_TILE], BF16)
        nc.vector.memset(zeros[:].bitcast(I32), 0)

        w_words = keep.tile([P, 2, 2 * E], U8, align_bytes=64)
        w_planes = keep.tile([P, 2, E], U8, align_bytes=64)
        nc.vector.memset(w_planes[:].bitcast(I32), 0)

        x_tiles = []
        for r in range(ROUNDS):
            x_tile = x_pool.tile([P, HOPS * K], BF16)
            x_tiles.append(x_tile)

        def load_x(r, first_hop, hops):
            nc.sync.dma_start(
                out=x_tiles[r][:, first_hop * K : (first_hop + hops) * K],
                in_=x[r * P : (r + 1) * P, first_hop : first_hop + hops, :].rearrange(
                    "n h k -> n (h k)"
                ),
            )

        def load_scales(operand):
            for quadrant in range(P // 32):
                nc.sync.dma_start(
                    out=w_planes[
                        32 * quadrant : 32 * quadrant + SCALE_ROWS, operand, :
                    ].bitcast(I32),
                    in_=given_scales[operand][
                        0, SCALE_ROWS * quadrant : SCALE_ROWS * (quadrant + 1), :
                    ].bitcast(I32),
                )

        def load_words(operand):
            nc.sync.dma_start(
                out=w_words[:, operand, :].bitcast(I32),
                in_=given_words[operand][0, :, :].bitcast(I32),
            )

        for hop in range(HOPS):
            load_x(0, hop, 1)
        load_x(1, 0, HOPS)
        load_scales(0)
        load_words(0)
        load_words(1)
        load_scales(1)
        for r in range(2, ROUNDS):
            load_x(r, 0, HOPS)

        sorted_words = {}

        def sort_round(r):
            tile = sort_pool.tile([P, HOPS * PAIRS], F32, name="sorted")
            nc.vector.tensor_copy(
                out=tile[:].rearrange("n (h u p) -> n u h p", h=HOPS, u=2),
                in_=x_tiles[r][:].bitcast(F32).rearrange("n (h p u) -> n u h p", h=HOPS, u=2),
            )
            sorted_words[r] = tile

        def transpose_hop(r, hop, bank):
            words = x_tiles[r][:].bitcast(F32)
            for u in range(2):
                if r in sorted_words:
                    start = hop * PAIRS + u * P
                    in_words = sorted_words[r][:, start : start + P]
                else:
                    in_words = words[:, hop * PAIRS + u : (hop + 1) * PAIRS : 2]
                nc.tensor.transpose(bank[:, u, :], in_words, identity[:])

        def warm_up(count):
            for i in range(count):
                idle = psum_o.tile([P, N_TILE], F32, name="acc")
                nc.tensor.matmul(idle[:], lhsT=zeros[:, 0:P], rhs=zeros[:], start=True, stop=True)

        def transpose_run(first_round):
            first = psum_t.tile([P, 2, 2, P], F32, name="bank_first")
            shared = psum_t.tile([P, 2, 2, P], F32, name="bank_shared")
            second = psum_t.tile([P, 2, 2, P], F32, name="bank_second")
            last_hops = [shared, shared]
            if first_round == 0:
                own = psum_o.tile([P, 2, 2, P], F32, name="acc")
                last_hops = [shared, own]
                warm_up(4)
            for hop in range(2):
                transpose_hop(first_round, hop, first[:, hop, :, :])
            for i in range(2):
                if first_round + i == 1:
                    warm_up(2)
                transpose_hop(first_round + i, 2, last_hops[i][:, i, :, :])
            for hop in range(2):
                transpose_hop(first_round + 1, hop, second[:, hop, :, :])
            return [
                (first[:], last_hops[0][:, 0:1, :, :]),
                (second[:], last_hops[1][:, 1:2, :, :]),
            ]

        def quantise(grouped, codes, planes, first_unit):
            units = slice(first_unit, first_unit + UNITS_PER_CALL)
            nc.vector.quantize_mx(
                out=codes[:, units, :].rearrange("p a i -> p (a i)").bitcast(FP8X4),
                scales=planes[:, units, :].rearrange("p a i -> p (a i)"),
                in_=grouped[:, units, :].rearrange("p a c -> p (a c)"),
            )

        def prepare_round(banks, copies, sort_between=()):
            grouped = prep.tile([P, UNITS, P * 4], BF16, align_bytes=64)
            for b, bank in enumerate(banks):
                first_hop = b * HOPS_PER_BANK
                hops_here = min(HOPS_PER_BANK, HOPS - first_hop)
                first_unit = X_UNITS[first_hop]
                copies[b](
                    out=grouped[:, first_unit : first_unit + hops_here, :]
                    .bitcast(F32)
                    .rearrange("p h (i u) -> p h i u", u=2),
                    in_=bank.rearrange("p h u i -> p h i u"),
                )
            codes = quantised.tile([P, UNITS, P], U32, align_bytes=64)
            planes = quantised.tile([P, UNITS, P], U8, align_bytes=64)
            halved = prep.tile([P, HOPS, P * 4], BF16)
            x_of_all = grouped[:, X_UNITS[0] : X_UNITS[0] + HOPS, :]
            for hops in (slice(0, 2), slice(2, HOPS)):
                nc.vector.tensor_scalar(
                    out=halved[:, hops, :], in0=x_of_all[:, hops, :], scalar1=0.5, scalar2=None, op0=MULT
                )
            quantise(grouped, codes, planes, X_UNITS[0])
            for r in sort_between[:1]:
                sort_round(r)
            nc.vector.tensor_tensor(
                out=grouped[:, NEIGH_UNITS[2] : NEIGH_UNITS[2] + 2, :],
                in0=halved[:, 0:2, :],
                in1=halved[:, 1:3, :],
                op=ADD,
            )
            for r in sort_between[1:]:
                sort_round(r)
            nc.vector.tensor_tensor(
                out=grouped[:, NEIGH_UNITS[1], :], in0=halved[:, 0, :], in1=halved[:, 2, :], op=ADD
            )
            quantise(grouped, codes, planes, NEIGH_UNITS[2])
            quantise(grouped, codes, planes, X_UNITS[2])
            return codes, planes

        def multiply_round(r, codes, planes):
            items = slice(r * P, (r + 1) * P)
            last_round = r == ROUNDS - 1
            result = results.tile([P, HOPS, E], F32)
            for hop in range(HOPS):
                accs = [psum_o.tile([P, N_TILE], F32, name="acc") for n in range(N_TILES)]
                if r == 0:
                    order = [(operand, n) for operand in range(2) for n in range(N_TILES)]
                else:
                    order = [(operand, n) for n in range(N_TILES) for operand in range(2)]
                for operand, n in order:
                    unit = (X_UNITS, NEIGH_UNITS)[operand][hop]
                    nc.tensor.matmul_mx(
                        out=accs[n][:],
                        lhsT=codes[:, unit, :].bitcast(FP8X4),
                        lhsT_scale=planes[:, unit, :],
                        rhs=w_words[
                            :, operand, 2 * N_TILE * n : 2 * N_TILE * (n + 1)
                        ].bitcast(FP4X4),
                        rhs_scale=w_planes[:, operand, N_TILE * n : N_TILE * (n + 1)],
                        start=(operand == 0),
                        stop=(operand == 1),
                    )
                for n in range(N_TILES):
                    cols = slice(N_TILE * n, N_TILE * (n + 1))
                    if n % 2 == 1 and (last_round or (r == ROUNDS - 2 and hop == HOPS - 1)):
                        nc.vector.tensor_copy(out=result[:, hop, cols], in_=accs[n][:])
                    else:
                        nc.scalar.copy(out=result[:, hop, cols], in_=accs[n][:])
                    if last_round and hop == HOPS - 1:
                        nc.sync.dma_start(out=out[items, hop, cols], in_=result[:, hop, cols])
                if not (last_round and hop == HOPS - 1):
                    nc.sync.dma_start(out=out[items, hop, :], in_=result[:, hop, :])

        ready = {}
        by_vector, by_scalar = nc.vector.tensor_copy, nc.scalar.copy

        banks = transpose_run(0)
        warm_up(1)
        ready[0] = prepare_round(banks[0], (by_vector, by_scalar))
        ready[1] = prepare_round(banks[1], (by_scalar, by_scalar), (2, 3))

        def prepare_rounds(first_round):
            banks = transpose_run(first_round)
            ready[first_round] = prepare_round(banks[0], (by_vector, by_vector))
            for r in range(first_round + RUN, min(first_round + 2 * RUN, ROUNDS)):
                sort_round(r)
            ready[first_round + 1] = prepare_round(banks[1], (by_vector, by_vector))

        for r in range(ROUNDS):
            multiply_round(r, ready[r][0], ready[r][1])
            if r % RUN == 0 and r + RUN < ROUNDS:
                prepare_rounds(r + RUN)
